import numpy as np
import ml_dtypes


def mxq(x, axis, fmt="e4m3"):
    dtype, down = {"e4m3": (ml_dtypes.float8_e4m3fn, 7), "e5m2": (ml_dtypes.float8_e5m2, 14)}[fmt]
    v = np.moveaxis(np.asarray(x, np.float32).astype(ml_dtypes.bfloat16).astype(np.float64), axis, -1)
    blocks = v.reshape(v.shape[:-1] + (-1, 32))
    amax = np.abs(blocks).max(-1, keepdims=True)
    byte = np.maximum(np.where(amax > 0, np.frexp(amax)[1] - 1 + 127, 0) - down, 1)
    scale = np.exp2(byte - 127.0)
    codes = (blocks / scale).astype(np.float32).astype(dtype).astype(np.float64)
    return np.moveaxis((codes * scale).reshape(v.shape), -1, axis)


WIDE = False


def mx_kscale(k):
    if not WIDE:
        return np.ones(k)
    levels = np.array([10, -10, 5, -5, 0])
    if k % 512:
        return np.exp2(np.random.permutation(np.resize(levels, k // 32))).repeat(32)
    a = np.empty((k // 512, 16))
    for p in range(k // 512):
        a[p, :8] = np.random.permutation(np.resize(levels, 8))
        for g in range(8):
            far = levels[np.abs(levels - a[p, g]) >= 10]
            a[p, g + 8] = far[np.random.randint(len(far))]
    return np.exp2(a.ravel()).repeat(32)


BF16 = ml_dtypes.bfloat16


def bf(x):
    return np.asarray(x, np.float32).astype(BF16)


def f64(x):
    return np.asarray(x).astype(np.float64)


B, IN, HID, CENT = 512, 128, 16384, 512


def setup_inputs():
    t = np.log2(mx_kscale(HID))
    a = t.max() - t
    sigmas = bf(1.0 + 0.1 * np.random.standard_normal(HID))
    c = np.random.standard_normal((HID, IN)) / np.sqrt(IN)
    c = c * np.sqrt(1.0 + a * np.log(2.0) / (f64(sigmas) ** 2 * (c * c).sum(1)))[:, None]
    return {"x": bf(np.random.standard_normal((B, IN)) / np.sqrt(IN)), "centres": bf(c), "sigmas": sigmas,
            "w1": bf(np.random.standard_normal((CENT, HID)) * 6.0 / np.sqrt(HID) * np.exp2(a)),
            "b1": bf(0.2 * np.random.standard_normal(CENT))}


def reference(x, centres, sigmas, w1, b1):
    x2 = np.sum(f64(x) * f64(x), axis=1, keepdims=True)
    c2 = np.sum(f64(centres) * f64(centres), axis=1)[None, :]
    d2 = np.maximum(x2 + c2 - 2.0 * (f64(x) @ f64(centres).T), 0.0)
    phi = np.exp(-d2 * (f64(sigmas) * f64(sigmas))[None, :])
    return np.maximum((mxq(phi, 1, "e4m3") @ mxq(f64(w1), 1, "e4m3").T) + f64(b1), 0.0)

@@ -1,0 +1,290 @@
+from contextlib import ExitStack
+
+import concourse.mybir as mybir
+from concourse.masks import make_identity
+
+F32 = mybir.dt.float32
+BF16 = mybir.dt.bfloat16
+U32 = mybir.dt.uint32
+U8 = mybir.dt.uint8
+FP8X4 = mybir.dt.float8_e4m3fn_x4
+ACT = mybir.ActivationFunctionType
+ALU = mybir.AluOpType
+
+P = 128
+B = 512
+IN = 128
+HID = 16384
+CENT = 512
+PACK = 4
+K_PASS = P * PACK
+ROUNDS = HID // K_PASS
+B_TILES = B // P
+C_TILES = CENT // P
+ROUNDS_PER_LOAD = 2
+W_LOAD = ROUNDS_PER_LOAD * K_PASS
+W_LOADS = HID // W_LOAD
+W_AHEAD = 3
+PAIRS = K_PASS // 2
+CEN_LOADS = 16
+GPSIMD_COLS = 384
+
+FLOPS = 2 * B * HID * (IN + CENT)
+
+
+def tile_networkprc_pa_k_kernel(tc, x, centres, sigmas, w1, b1, out):
+    nc = tc.nc
+    with ExitStack() as ctx:
+        const = ctx.enter_context(tc.tile_pool(name="const", bufs=1))
+        wload = ctx.enter_context(tc.tile_pool(name="wload", bufs=W_AHEAD + 1))
+        wgroup = ctx.enter_context(tc.tile_pool(name="wgroup", bufs=3))
+        wcodes = ctx.enter_context(tc.tile_pool(name="wcodes", bufs=6))
+        pcodes = ctx.enter_context(tc.tile_pool(name="pcodes", bufs=3))
+        cpool = ctx.enter_context(tc.tile_pool(name="cpool", bufs=4))
+        junk = ctx.enter_context(tc.tile_pool(name="junk", bufs=2))
+        dpool = ctx.enter_context(tc.tile_pool(name="dpool", bufs=4))
+        phpool = ctx.enter_context(tc.tile_pool(name="phpool", bufs=3))
+        gpool = ctx.enter_context(tc.tile_pool(name="gpool", bufs=1))
+        accps = ctx.enter_context(tc.psum_pool(name="accps", bufs=1))
+        spsum = ctx.enter_context(tc.psum_pool(name="spsum", bufs=2))
+        tpsum = ctx.enter_context(tc.psum_pool(name="tpsum", bufs=2))
+        ctx.enter_context(tc.manual_schedule())
+
+        w1_v = w1.rearrange("(ct c) j -> c ct j", c=P)
+        cen_v = centres.rearrange("(r p t) k -> p r t k", p=P, t=PACK)
+        out_v = out.rearrange("(p a) c -> p a c", a=B_TILES)
+
+        w_sb = {}
+        wT_ps = {}
+        wgrp = {}
+        w_codes = {}
+        w_scales = {}
+        cT_ps = {}
+        cT = {}
+        c2 = {}
+        s_ps = {}
+        d2 = {}
+        ph = {}
+        grp = {}
+        p_codes = {}
+        p_scales = {}
+
+        ident_bf = const.tile([P, P], BF16)
+        make_identity(nc, ident_bf[:])
+        ident_f32 = const.tile([P, P], F32)
+        make_identity(nc, ident_f32[:])
+        quarter = const.tile([P, P], F32)
+        nc.vector.memset(quarter[:], 0.25)
+
+        def load_w(n):
+            w_sb[n] = wload.tile([P, C_TILES, W_LOAD], BF16, name="w_sb", tag="w_sb")
+            nc.sync.dma_start(out=w_sb[n][:], in_=w1_v[:, :, n * W_LOAD : (n + 1) * W_LOAD])
+
+        def load_centres(n):
+            step = ROUNDS // CEN_LOADS
+            nc.sync.dma_start(
+                out=cen_sb[:, n * step : (n + 1) * step, :, :],
+                in_=cen_v[:, n * step : (n + 1) * step, :, :],
+            )
+
+        def w_transposes(r):
+            n = r // ROUNDS_PER_LOAD
+            if r % ROUNDS_PER_LOAD == 0 and n + W_AHEAD < W_LOADS:
+                load_w(n + W_AHEAD)
+            first_word = (r % ROUNDS_PER_LOAD) * PAIRS
+            for h in range(2):
+                wT_ps[r, h] = tpsum.tile([P, 2, 2 * P], F32, name="wT_ps", tag="t_ps")
+                for u in range(2):
+                    for q in range(2):
+                        words = w_sb[n][:, 2 * h + q, :].bitcast(F32)
+                        nc.tensor.transpose(
+                            wT_ps[r, h][:, u, q * P : (q + 1) * P],
+                            words[:, first_word + u : first_word + PAIRS : 2],
+                            ident_f32[:],
+                        )
+
+        def w_copies(r):
+            wgrp[r] = wgroup.tile([P, CENT * PACK], BF16, name="wgrp", tag="wgrp", align_bytes=64)
+            words = wgrp[r][:].bitcast(F32).rearrange("p (c u) -> p c u", u=2)
+            for h in range(2):
+                nc.scalar.copy(
+                    out=words[:, h * 2 * P : (h + 1) * 2 * P, :],
+                    in_=wT_ps[r, h][:].rearrange("p u c -> p c u"),
+                )
+
+        def w_quantise(r):
+            w_codes[r] = wcodes.tile([P, CENT], U32, name="w_codes", tag="w_codes", align_bytes=64)
+            w_scales[r] = wcodes.tile([P, CENT], U8, name="w_scales", tag="w_scales", align_bytes=64)
+            nc.vector.quantize_mx(out=w_codes[r][:].bitcast(FP8X4), scales=w_scales[r][:], in_=wgrp[r][:])
+
+        def centre_tile(r, t):
+            return cen_sb[:, r, t, :]
+
+        def c_transposes(r):
+            cT_ps[r] = tpsum.tile([P, PACK, P], BF16, name="cT_ps", tag="t_ps")
+            for t in range(PACK):
+                nc.tensor.transpose(cT_ps[r][:, t, :], centre_tile(r, t), ident_bf[:])
+
+        def c_copy(r):
+            cT[r] = cpool.tile([P, PACK, P], BF16, name="cT", tag="cT")
+            nc.vector.tensor_copy(out=cT[r][:], in_=cT_ps[r][:])
+
+        def c_norms(r):
+            c2[r] = cpool.tile([P, PACK], F32, name="c2", tag="c2")
+            squares = junk.tile([P, PACK, IN], BF16)
+            for t in range(PACK):
+                nc.scalar.activation(
+                    out=squares[:, t, :], in_=centre_tile(r, t), func=ACT.Square, accum_out=c2[r][:, t : t + 1]
+                )
+
+        def products(r, t):
+            s_ps[r, t] = spsum.tile([P, B], F32, name="s_ps", tag="s_ps")
+            nc.tensor.matmul(s_ps[r, t][:], lhsT=cT[r][:, t, :], rhs=xT2[:], start=True, stop=True)
+
+        def distances(r, t):
+            d2[r, t] = dpool.tile([P, B], F32, name="d2", tag="d2")
+            nc.vector.scalar_tensor_tensor(
+                out=d2[r, t][:],
+                in0=x2[:],
+                scalar=c2[r][:, t : t + 1],
+                in1=s_ps[r, t][:],
+                op0=ALU.add,
+                op1=ALU.subtract,
+            )
+
+        def exponentials(r, t):
+            if t == 0:
+                ph[r] = phpool.tile([P, PACK, B], BF16, name="ph", tag="ph")
+            col = PACK * r + t
+            nc.scalar.activation(out=ph[r][:, t, :], in_=d2[r, t][:], func=ACT.Exp, scale=negs2[:, col : col + 1])
+
+        def regroup(r):
+            grp[r] = gpool.tile([P, B, PACK], BF16, name="grp", tag="grp", align_bytes=64)
+            nc.vector.tensor_scalar(
+                out=grp[r][:, GPSIMD_COLS:B, :].rearrange("p (c i) t -> p c t i", i=4),
+                in0=ph[r][:, :, GPSIMD_COLS:B].rearrange("p t (c i) -> p c t i", i=4),
+                scalar1=1.0,
+                scalar2=None,
+                op0=ALU.min,
+            )
+            nc.gpsimd.tensor_scalar(
+                out=grp[r][:, 0:GPSIMD_COLS, :],
+                in0=ph[r][:, :, 0:GPSIMD_COLS].rearrange("p t n -> p n t"),
+                scalar1=1.0,
+                scalar2=0.0,
+                op0=ALU.min,
+                op1=ALU.max,
+            )
+
+        def p_quantise(r):
+            p_codes[r] = pcodes.tile([P, B], U32, name="p_codes", tag="p_codes", align_bytes=64)
+            p_scales[r] = pcodes.tile([P, B], U8, name="p_scales", tag="p_scales", align_bytes=64)
+            nc.vector.quantize_mx(
+                out=p_codes[r][:].bitcast(FP8X4), scales=p_scales[r][:], in_=grp[r][:].rearrange("p n t -> p (n t)")
+            )
+
+        def mx_passes(r):
+            for a in range(B_TILES):
+                nc.tensor.matmul_mx(
+                    out=acc[a][:],
+                    lhsT=p_codes[r][:, a * P : (a + 1) * P].bitcast(FP8X4),
+                    lhsT_scale=p_scales[r][:, a * P : (a + 1) * P],
+                    rhs=w_codes[r][:].bitcast(FP8X4),
+                    rhs_scale=w_scales[r][:],
+                    start=(r == 0),
+                    stop=(r == ROUNDS - 1),
+                )
+
+        x_sb = const.tile([P, B_TILES, IN], BF16)
+        nc.sync.dma_start(out=x_sb[:], in_=x.rearrange("(p a) k -> p a k", a=B_TILES))
+        cen_sb = const.tile([P, ROUNDS, PACK, IN], BF16)
+        load_centres(0)
+        sig_nat = const.tile([P, K_PASS], BF16)
+        nc.vector.memset(sig_nat[:], 0.0)
+        nc.sync.dma_start(out=sig_nat[0:ROUNDS, :], in_=sigmas.rearrange("(r w) -> r w", w=K_PASS))
+        load_w(0)
+        load_centres(1)
+        for n in range(1, W_AHEAD):
+            load_w(n)
+        for n in range(2, CEN_LOADS):
+            load_centres(n)
+        b1_bc = const.tile([P, CENT], BF16)
+        nc.sync.dma_start(out=b1_bc[:], in_=b1.partition_broadcast(P))
+
+        xT_ps = tpsum.tile([P, B_TILES, P], BF16, tag="t_ps")
+        for a in range(B_TILES):
+            nc.tensor.transpose(xT_ps[:, a, :], x_sb[:, a, :], ident_bf[:])
+        xT2 = const.tile([P, B], BF16)
+        nc.scalar.mul(out=xT2[:], in_=xT_ps[:].rearrange("p a i -> p (a i)"), mul=2.0)
+        xsq = const.tile([P, B], F32)
+        nc.vector.tensor_tensor(out=xsq[:], in0=xT2[:], in1=xT2[:], op=ALU.mult)
+
+        c_transposes(0)
+        c_copy(0)
+        c_norms(0)
+
+        sigT_ps = tpsum.tile([P, 2, P], F32, tag="t_ps")
+        for u in range(2):
+            nc.tensor.transpose(sigT_ps[:, u, :], sig_nat[:].bitcast(F32)[:, u:PAIRS:2], ident_f32[:])
+        sigT = const.tile([P, P], BF16)
+        nc.vector.tensor_copy(
+            out=sigT[:].bitcast(F32).rearrange("p (r u) -> p r u", u=2),
+            in_=sigT_ps[:, :, 0:ROUNDS].rearrange("p u r -> p r u"),
+        )
+        negs2 = const.tile([P, P], F32)
+        nc.vector.scalar_tensor_tensor(
+            out=negs2[:], in0=sigT[:], scalar=-1.0, in1=sigT[:], op0=ALU.mult, op1=ALU.mult
+        )
+
+        x2_ps = spsum.tile([P, B], F32, tag="s_ps")
+        nc.tensor.matmul(x2_ps[:], lhsT=quarter[:], rhs=xsq[:], start=True, stop=True)
+        x2 = const.tile([P, B], F32)
+        nc.vector.tensor_copy(out=x2[:], in_=x2_ps[:])
+
+        acc = [accps.tile([P, CENT], F32, name="acc%d" % a) for a in range(B_TILES)]
+
+        products(0, 0)
+        products(0, 1)
+        c_transposes(1)
+        c_copy(1)
+        c_norms(1)
+        w_transposes(0)
+        w_copies(0)
+
+        for i in range(ROUNDS + 3):
+            if i < ROUNDS:
+                distances(i, 0)
+                distances(i, 1)
+                products(i, 2)
+                products(i, 3)
+                exponentials(i, 0)
+                exponentials(i, 1)
+                w_quantise(i)
+            if 0 <= i - 2 < ROUNDS:
+                p_quantise(i - 2)
+            if 0 <= i - 1 < ROUNDS:
+                regroup(i - 1)
+            if i + 1 < ROUNDS:
+                w_transposes(i + 1)
+                w_copies(i + 1)
+            if i + 2 < ROUNDS:
+                c_transposes(i + 2)
+            if i < ROUNDS:
+                distances(i, 2)
+                distances(i, 3)
+                exponentials(i, 2)
+                exponentials(i, 3)
+            if i + 2 < ROUNDS:
+                c_copy(i + 2)
+                c_norms(i + 2)
+            if i + 1 < ROUNDS:
+                products(i + 1, 0)
+                products(i + 1, 1)
+            if 0 <= i - 3 < ROUNDS:
+                mx_passes(i - 3)
+
+        res = const.tile([P, B_TILES, CENT], F32)
+        for a in range(B_TILES):
+            nc.vector.tensor_tensor(out=res[:, a, :], in0=acc[a][:], in1=b1_bc[:], op=ALU.add)
+            nc.scalar.activation(out=res[:, a, :], in_=res[:, a, :], func=ACT.Relu)
+            nc.sync.dma_start(out=out_v[:, a, :], in_=res[:, a, :])

@@ -41,8 +41,8 @@ def tile_networkprc_pa_k_kernel(tc, x, centres, sigmas, w1, b1, out):
         wcodes = ctx.enter_context(tc.tile_pool(name="wcodes", bufs=6))
         pcodes = ctx.enter_context(tc.tile_pool(name="pcodes", bufs=3))
         cpool = ctx.enter_context(tc.tile_pool(name="cpool", bufs=4))
-        junk = ctx.enter_context(tc.tile_pool(name="junk", bufs=2))
-        dpool = ctx.enter_context(tc.tile_pool(name="dpool", bufs=4))
+        junk = ctx.enter_context(tc.tile_pool(name="junk", bufs=4))
+        dpool = ctx.enter_context(tc.tile_pool(name="dpool", bufs=6))
         phpool = ctx.enter_context(tc.tile_pool(name="phpool", bufs=3))
         gpool = ctx.enter_context(tc.tile_pool(name="gpool", bufs=1))
         accps = ctx.enter_context(tc.psum_pool(name="accps", bufs=1))
@@ -87,30 +87,29 @@ def tile_networkprc_pa_k_kernel(tc, x, centres, sigmas, w1, b1, out):
                 in_=cen_v[:, n * step : (n + 1) * step, :, :],
             )
 
-        def w_transposes(r):
+        def w_transposes(r, h):
             n = r // ROUNDS_PER_LOAD
-            if r % ROUNDS_PER_LOAD == 0 and n + W_AHEAD < W_LOADS:
+            if h == 0 and r % ROUNDS_PER_LOAD == 0 and n + W_AHEAD < W_LOADS:
                 load_w(n + W_AHEAD)
             first_word = (r % ROUNDS_PER_LOAD) * PAIRS
-            for h in range(2):
-                wT_ps[r, h] = tpsum.tile([P, 2, 2 * P], F32, name="wT_ps", tag="t_ps")
-                for u in range(2):
-                    for q in range(2):
-                        words = w_sb[n][:, 2 * h + q, :].bitcast(F32)
-                        nc.tensor.transpose(
-                            wT_ps[r, h][:, u, q * P : (q + 1) * P],
-                            words[:, first_word + u : first_word + PAIRS : 2],
-                            ident_f32[:],
-                        )
+            wT_ps[r, h] = tpsum.tile([P, 2, 2 * P], F32, name="wT_ps", tag="t_ps")
+            for u in range(2):
+                for q in range(2):
+                    words = w_sb[n][:, 2 * h + q, :].bitcast(F32)
+                    nc.tensor.transpose(
+                        wT_ps[r, h][:, u, q * P : (q + 1) * P],
+                        words[:, first_word + u : first_word + PAIRS : 2],
+                        ident_f32[:],
+                    )
 
-        def w_copies(r):
-            wgrp[r] = wgroup.tile([P, CENT * PACK], BF16, name="wgrp", tag="wgrp", align_bytes=64)
+        def w_copy(r, h):
+            if h == 0:
+                wgrp[r] = wgroup.tile([P, CENT * PACK], BF16, name="wgrp", tag="wgrp", align_bytes=64)
             words = wgrp[r][:].bitcast(F32).rearrange("p (c u) -> p c u", u=2)
-            for h in range(2):
-                nc.scalar.copy(
-                    out=words[:, h * 2 * P : (h + 1) * 2 * P, :],
-                    in_=wT_ps[r, h][:].rearrange("p u c -> p c u"),
-                )
+            nc.scalar.copy(
+                out=words[:, h * 2 * P : (h + 1) * 2 * P, :],
+                in_=wT_ps[r, h][:].rearrange("p u c -> p c u"),
+            )
 
         def w_quantise(r):
             w_codes[r] = wcodes.tile([P, CENT], U32, name="w_codes", tag="w_codes", align_bytes=64)
@@ -129,13 +128,13 @@ def tile_networkprc_pa_k_kernel(tc, x, centres, sigmas, w1, b1, out):
             cT[r] = cpool.tile([P, PACK, P], BF16, name="cT", tag="cT")
             nc.vector.tensor_copy(out=cT[r][:], in_=cT_ps[r][:])
 
-        def c_norms(r):
-            c2[r] = cpool.tile([P, PACK], F32, name="c2", tag="c2")
-            squares = junk.tile([P, PACK, IN], BF16)
-            for t in range(PACK):
-                nc.scalar.activation(
-                    out=squares[:, t, :], in_=centre_tile(r, t), func=ACT.Square, accum_out=c2[r][:, t : t + 1]
-                )
+        def c_norm(r, t):
+            if t == 0:
+                c2[r] = cpool.tile([P, PACK], F32, name="c2", tag="c2")
+            squares = junk.tile([P, IN], BF16, name="squares", tag="squares")
+            nc.scalar.activation(
+                out=squares[:], in_=centre_tile(r, t), func=ACT.Square, accum_out=c2[r][:, t : t + 1]
+            )
 
         def products(r, t):
             s_ps[r, t] = spsum.tile([P, B], F32, name="s_ps", tag="s_ps")
@@ -219,10 +218,6 @@ def tile_networkprc_pa_k_kernel(tc, x, centres, sigmas, w1, b1, out):
         xsq = const.tile([P, B], F32)
         nc.vector.tensor_tensor(out=xsq[:], in0=xT2[:], in1=xT2[:], op=ALU.mult)
 
-        c_transposes(0)
-        c_copy(0)
-        c_norms(0)
-
         sigT_ps = tpsum.tile([P, 2, P], F32, tag="t_ps")
         for u in range(2):
             nc.tensor.transpose(sigT_ps[:, u, :], sig_nat[:].bitcast(F32)[:, u:PAIRS:2], ident_f32[:])
@@ -243,45 +238,37 @@ def tile_networkprc_pa_k_kernel(tc, x, centres, sigmas, w1, b1, out):
 
         acc = [accps.tile([P, CENT], F32, name="acc%d" % a) for a in range(B_TILES)]
 
-        products(0, 0)
-        products(0, 1)
-        c_transposes(1)
-        c_copy(1)
-        c_norms(1)
-        w_transposes(0)
-        w_copies(0)
-
-        for i in range(ROUNDS + 3):
-            if i < ROUNDS:
-                distances(i, 0)
-                distances(i, 1)
-                products(i, 2)
-                products(i, 3)
-                exponentials(i, 0)
-                exponentials(i, 1)
-                w_quantise(i)
-            if 0 <= i - 2 < ROUNDS:
-                p_quantise(i - 2)
-            if 0 <= i - 1 < ROUNDS:
-                regroup(i - 1)
-            if i + 1 < ROUNDS:
-                w_transposes(i + 1)
-                w_copies(i + 1)
-            if i + 2 < ROUNDS:
-                c_transposes(i + 2)
-            if i < ROUNDS:
-                distances(i, 2)
-                distances(i, 3)
-                exponentials(i, 2)
-                exponentials(i, 3)
-            if i + 2 < ROUNDS:
-                c_copy(i + 2)
-                c_norms(i + 2)
-            if i + 1 < ROUNDS:
-                products(i + 1, 0)
-                products(i + 1, 1)
-            if 0 <= i - 3 < ROUNDS:
-                mx_passes(i - 3)
+        for i in range(-2, ROUNDS + 5):
+            for stage, r, part in (
+                (mx_passes, i - 5, ()),
+                (products, i - 1, (3,)),
+                (products, i, (0,)),
+                (p_quantise, i - 3, ()),
+                (w_quantise, i - 1, ()),
+                (regroup, i - 2, ()),
+                (distances, i - 1, (3,)),
+                (distances, i, (0,)),
+                (exponentials, i - 1, (0,)),
+                (c_norm, i + 1, (0,)),
+                (c_norm, i + 1, (1,)),
+                (w_copy, i, (1,)),
+                (w_transposes, i + 1, (0,)),
+                (c_transposes, i + 2, ()),
+                (products, i, (1,)),
+                (products, i, (2,)),
+                (c_copy, i + 2, ()),
+                (distances, i, (1,)),
+                (distances, i, (2,)),
+                (exponentials, i - 1, (1,)),
+                (c_norm, i + 1, (2,)),
+                (exponentials, i - 1, (2,)),
+                (w_copy, i + 1, (0,)),
+                (w_transposes, i + 1, (1,)),
+                (c_norm, i + 1, (3,)),
+                (exponentials, i - 1, (3,)),
+            ):
+                if 0 <= r < ROUNDS:
+                    stage(r, *part)
 
         res = const.tile([P, B_TILES, CENT], F32)
         for a in range(B_TILES):

@@ -21,13 +21,12 @@ K_PASS = P * PACK
 ROUNDS = HID // K_PASS
 B_TILES = B // P
 C_TILES = CENT // P
-ROUNDS_PER_LOAD = 2
-W_LOAD = ROUNDS_PER_LOAD * K_PASS
-W_LOADS = HID // W_LOAD
-W_AHEAD = 3
+W_AHEAD = 6
 PAIRS = K_PASS // 2
 CEN_LOADS = 16
-GPSIMD_COLS = 384
+NORMS_AHEAD = 24
+VECTOR_ROUNDS = 2
+GPSIMD_COLS = 416
 
 FLOPS = 2 * B * HID * (IN + CENT)
 
@@ -61,7 +60,6 @@ def tile_networkprc_pa_k_kernel(tc, x, centres, sigmas, w1, b1, out):
         w_scales = {}
         cT_ps = {}
         cT = {}
-        c2 = {}
         s_ps = {}
         d2 = {}
         ph = {}
@@ -73,12 +71,10 @@ def tile_networkprc_pa_k_kernel(tc, x, centres, sigmas, w1, b1, out):
         make_identity(nc, ident_bf[:])
         ident_f32 = const.tile([P, P], F32)
         make_identity(nc, ident_f32[:])
-        quarter = const.tile([P, P], F32)
-        nc.vector.memset(quarter[:], 0.25)
 
-        def load_w(n):
-            w_sb[n] = wload.tile([P, C_TILES, W_LOAD], BF16, name="w_sb", tag="w_sb")
-            nc.sync.dma_start(out=w_sb[n][:], in_=w1_v[:, :, n * W_LOAD : (n + 1) * W_LOAD])
+        def load_w(r):
+            w_sb[r] = wload.tile([P, C_TILES, K_PASS], BF16, name="w_sb", tag="w_sb")
+            nc.sync.dma_start(out=w_sb[r][:], in_=w1_v[:, :, r * K_PASS : (r + 1) * K_PASS])
 
         def load_centres(n):
             step = ROUNDS // CEN_LOADS
@@ -88,18 +84,14 @@ def tile_networkprc_pa_k_kernel(tc, x, centres, sigmas, w1, b1, out):
             )
 
         def w_transposes(r, h):
-            n = r // ROUNDS_PER_LOAD
-            if h == 0 and r % ROUNDS_PER_LOAD == 0 and n + W_AHEAD < W_LOADS:
-                load_w(n + W_AHEAD)
-            first_word = (r % ROUNDS_PER_LOAD) * PAIRS
+            if h == 0 and r + W_AHEAD < ROUNDS:
+                load_w(r + W_AHEAD)
             wT_ps[r, h] = tpsum.tile([P, 2, 2 * P], F32, name="wT_ps", tag="t_ps")
             for u in range(2):
                 for q in range(2):
-                    words = w_sb[n][:, 2 * h + q, :].bitcast(F32)
+                    words = w_sb[r][:, 2 * h + q, :].bitcast(F32)
                     nc.tensor.transpose(
-                        wT_ps[r, h][:, u, q * P : (q + 1) * P],
-                        words[:, first_word + u : first_word + PAIRS : 2],
-                        ident_f32[:],
+                        wT_ps[r, h][:, u, q * P : (q + 1) * P], words[:, u:PAIRS:2], ident_f32[:]
                     )
 
         def w_copy(r, h):
@@ -128,13 +120,17 @@ def tile_networkprc_pa_k_kernel(tc, x, centres, sigmas, w1, b1, out):
             cT[r] = cpool.tile([P, PACK, P], BF16, name="cT", tag="cT")
             nc.vector.tensor_copy(out=cT[r][:], in_=cT_ps[r][:])
 
-        def c_norm(r, t):
-            if t == 0:
-                c2[r] = cpool.tile([P, PACK], F32, name="c2", tag="c2")
+        def c_norm(n):
             squares = junk.tile([P, IN], BF16, name="squares", tag="squares")
             nc.scalar.activation(
-                out=squares[:], in_=centre_tile(r, t), func=ACT.Square, accum_out=c2[r][:, t : t + 1]
+                out=squares[:], in_=centre_tile(n // PACK, n % PACK), func=ACT.Square, accum_out=c2[:, n : n + 1]
             )
+
+        def norms(i, k):
+            left = ROUNDS * PACK - NORMS_AHEAD
+            first, last = (NORMS_AHEAD + left * j // (ROUNDS - 1) for j in (i, i + 1))
+            for n in range(first + k, min(last, ROUNDS * PACK), 3):
+                c_norm(n)
 
         def products(r, t):
             s_ps[r, t] = spsum.tile([P, B], F32, name="s_ps", tag="s_ps")
@@ -145,7 +141,7 @@ def tile_networkprc_pa_k_kernel(tc, x, centres, sigmas, w1, b1, out):
             nc.vector.scalar_tensor_tensor(
                 out=d2[r, t][:],
                 in0=x2[:],
-                scalar=c2[r][:, t : t + 1],
+                scalar=c2[:, PACK * r + t : PACK * r + t + 1],
                 in1=s_ps[r, t][:],
                 op0=ALU.add,
                 op1=ALU.subtract,
@@ -159,16 +155,19 @@ def tile_networkprc_pa_k_kernel(tc, x, centres, sigmas, w1, b1, out):
 
         def regroup(r):
             grp[r] = gpool.tile([P, B, PACK], BF16, name="grp", tag="grp", align_bytes=64)
+            cut = GPSIMD_COLS if r < ROUNDS - VECTOR_ROUNDS else 0
             nc.vector.tensor_scalar(
-                out=grp[r][:, GPSIMD_COLS:B, :].rearrange("p (c i) t -> p c t i", i=4),
-                in0=ph[r][:, :, GPSIMD_COLS:B].rearrange("p t (c i) -> p c t i", i=4),
+                out=grp[r][:, cut:B, :].rearrange("p (c i) t -> p c t i", i=4),
+                in0=ph[r][:, :, cut:B].rearrange("p t (c i) -> p c t i", i=4),
                 scalar1=1.0,
                 scalar2=None,
                 op0=ALU.min,
             )
+            if cut == 0:
+                return
             nc.gpsimd.tensor_scalar(
-                out=grp[r][:, 0:GPSIMD_COLS, :],
-                in0=ph[r][:, :, 0:GPSIMD_COLS].rearrange("p t n -> p n t"),
+                out=grp[r][:, 0:cut, :],
+                in0=ph[r][:, :, 0:cut].rearrange("p t n -> p n t"),
                 scalar1=1.0,
                 scalar2=0.0,
                 op0=ALU.min,
@@ -201,26 +200,47 @@ def tile_networkprc_pa_k_kernel(tc, x, centres, sigmas, w1, b1, out):
         sig_nat = const.tile([P, K_PASS], BF16)
         nc.vector.memset(sig_nat[:], 0.0)
         nc.sync.dma_start(out=sig_nat[0:ROUNDS, :], in_=sigmas.rearrange("(r w) -> r w", w=K_PASS))
-        load_w(0)
         load_centres(1)
+        load_w(0)
+        load_centres(2)
         for n in range(1, W_AHEAD):
+            load_centres(n + 2)
             load_w(n)
-        for n in range(2, CEN_LOADS):
+        for n in range(W_AHEAD + 2, CEN_LOADS):
             load_centres(n)
         b1_bc = const.tile([P, CENT], BF16)
         nc.sync.dma_start(out=b1_bc[:], in_=b1.partition_broadcast(P))
+
+        c2 = const.tile([P, ROUNDS * PACK], F32)
 
         xT_ps = tpsum.tile([P, B_TILES, P], BF16, tag="t_ps")
         for a in range(B_TILES):
             nc.tensor.transpose(xT_ps[:, a, :], x_sb[:, a, :], ident_bf[:])
         xT2 = const.tile([P, B], BF16)
-        nc.scalar.mul(out=xT2[:], in_=xT_ps[:].rearrange("p a i -> p (a i)"), mul=2.0)
-        xsq = const.tile([P, B], F32)
-        nc.vector.tensor_tensor(out=xsq[:], in0=xT2[:], in1=xT2[:], op=ALU.mult)
+        nc.vector.tensor_scalar(
+            out=xT2[:], in0=xT_ps[:].rearrange("p a i -> p (a i)"), scalar1=2.0, scalar2=None, op0=ALU.mult
+        )
+        x2col = const.tile([P, B_TILES], F32)
+        for a in range(B_TILES):
+            squares = junk.tile([P, IN], BF16, name="squares", tag="squares")
+            nc.scalar.activation(out=squares[:], in_=x_sb[:, a, :], func=ACT.Square, accum_out=x2col[:, a : a + 1])
+        c_transposes(0)
+        c_copy(0)
+        for n in range(PACK):
+            c_norm(n)
+
+        x2_ps = spsum.tile([P, B], F32, tag="s_ps")
+        for a in range(B_TILES):
+            nc.tensor.transpose(x2_ps[:, a * P : (a + 1) * P], x2col[:, a : a + 1].to_broadcast([P, P]), ident_f32[:])
+        x2 = const.tile([P, B], F32)
+        nc.vector.tensor_copy(out=x2[:], in_=x2_ps[:])
+
+        products(0, 0)
 
         sigT_ps = tpsum.tile([P, 2, P], F32, tag="t_ps")
         for u in range(2):
             nc.tensor.transpose(sigT_ps[:, u, :], sig_nat[:].bitcast(F32)[:, u:PAIRS:2], ident_f32[:])
+        distances(0, 0)
         sigT = const.tile([P, P], BF16)
         nc.vector.tensor_copy(
             out=sigT[:].bitcast(F32).rearrange("p (r u) -> p r u", u=2),
@@ -231,28 +251,27 @@ def tile_networkprc_pa_k_kernel(tc, x, centres, sigmas, w1, b1, out):
             out=negs2[:], in0=sigT[:], scalar=-1.0, in1=sigT[:], op0=ALU.mult, op1=ALU.mult
         )
 
-        x2_ps = spsum.tile([P, B], F32, tag="s_ps")
-        nc.tensor.matmul(x2_ps[:], lhsT=quarter[:], rhs=xsq[:], start=True, stop=True)
-        x2 = const.tile([P, B], F32)
-        nc.vector.tensor_copy(out=x2[:], in_=x2_ps[:])
+        for n in range(PACK, NORMS_AHEAD):
+            c_norm(n)
+        c_transposes(1)
+        c_copy(1)
 
         acc = [accps.tile([P, CENT], F32, name="acc%d" % a) for a in range(B_TILES)]
 
-        for i in range(-2, ROUNDS + 5):
+        for i in range(ROUNDS + 5):
             for stage, r, part in (
                 (mx_passes, i - 5, ()),
                 (products, i - 1, (3,)),
                 (products, i, (0,)),
                 (p_quantise, i - 3, ()),
-                (w_quantise, i - 1, ()),
+                (w_quantise, i - 2, ()),
                 (regroup, i - 2, ()),
                 (distances, i - 1, (3,)),
                 (distances, i, (0,)),
                 (exponentials, i - 1, (0,)),
-                (c_norm, i + 1, (0,)),
-                (c_norm, i + 1, (1,)),
-                (w_copy, i, (1,)),
-                (w_transposes, i + 1, (0,)),
+                (norms, i, (0,)),
+                (w_copy, i - 1, (1,)),
+                (w_transposes, i, (0,)),
                 (c_transposes, i + 2, ()),
                 (products, i, (1,)),
                 (products, i, (2,)),
@@ -260,14 +279,15 @@ def tile_networkprc_pa_k_kernel(tc, x, centres, sigmas, w1, b1, out):
                 (distances, i, (1,)),
                 (distances, i, (2,)),
                 (exponentials, i - 1, (1,)),
-                (c_norm, i + 1, (2,)),
+                (norms, i, (1,)),
                 (exponentials, i - 1, (2,)),
-                (w_copy, i + 1, (0,)),
-                (w_transposes, i + 1, (1,)),
-                (c_norm, i + 1, (3,)),
+                (w_copy, i, (0,)),
+                (w_transposes, i, (1,)),
+                (norms, i, (2,)),
                 (exponentials, i - 1, (3,)),
             ):
-                if 0 <= r < ROUNDS:
+                ahead = r == 0 and part == (0,) and stage in (products, distances)
+                if 0 <= r < ROUNDS and not ahead:
                     stage(r, *part)
 
         res = const.tile([P, B_TILES, CENT], F32)

@@ -153,16 +153,19 @@ def tile_networkprc_pa_k_kernel(tc, x, centres, sigmas, w1, b1, out):
             col = PACK * r + t
             nc.scalar.activation(out=ph[r][:, t, :], in_=d2[r, t][:], func=ACT.Exp, scale=negs2[:, col : col + 1])
 
-        def regroup(r):
-            grp[r] = gpool.tile([P, B, PACK], BF16, name="grp", tag="grp", align_bytes=64)
-            cut = GPSIMD_COLS if r < ROUNDS - VECTOR_ROUNDS else 0
+        def regroup_vector(r, first, last):
             nc.vector.tensor_scalar(
-                out=grp[r][:, cut:B, :].rearrange("p (c i) t -> p c t i", i=4),
-                in0=ph[r][:, :, cut:B].rearrange("p t (c i) -> p c t i", i=4),
+                out=grp[r][:, first:last, :].rearrange("p (c i) t -> p c t i", i=4),
+                in0=ph[r][:, :, first:last].rearrange("p t (c i) -> p c t i", i=4),
                 scalar1=1.0,
                 scalar2=None,
                 op0=ALU.min,
             )
+
+        def regroup(r):
+            cut = GPSIMD_COLS if r < ROUNDS - VECTOR_ROUNDS else 0
+            grp[r] = gpool.tile([P, B, PACK], BF16, name="grp", tag="grp", align_bytes=64)
+            regroup_vector(r, cut, B)
             if cut == 0:
                 return
             nc.gpsimd.tensor_scalar(
@@ -181,17 +184,29 @@ def tile_networkprc_pa_k_kernel(tc, x, centres, sigmas, w1, b1, out):
                 out=p_codes[r][:].bitcast(FP8X4), scales=p_scales[r][:], in_=grp[r][:].rearrange("p n t -> p (n t)")
             )
 
+        def quantise_block(r, a):
+            cols = slice(a * P, (a + 1) * P)
+            nc.vector.quantize_mx(
+                out=p_codes[r][:, cols].bitcast(FP8X4),
+                scales=p_scales[r][:, cols],
+                in_=grp[r][:, cols, :].rearrange("p n t -> p (n t)"),
+            )
+
+        def mx_pass(r, a):
+            cols = slice(a * P, (a + 1) * P)
+            nc.tensor.matmul_mx(
+                out=acc[a][:],
+                lhsT=p_codes[r][:, cols].bitcast(FP8X4),
+                lhsT_scale=p_scales[r][:, cols],
+                rhs=w_codes[r][:].bitcast(FP8X4),
+                rhs_scale=w_scales[r][:],
+                start=(r == 0),
+                stop=(r == ROUNDS - 1),
+            )
+
         def mx_passes(r):
             for a in range(B_TILES):
-                nc.tensor.matmul_mx(
-                    out=acc[a][:],
-                    lhsT=p_codes[r][:, a * P : (a + 1) * P].bitcast(FP8X4),
-                    lhsT_scale=p_scales[r][:, a * P : (a + 1) * P],
-                    rhs=w_codes[r][:].bitcast(FP8X4),
-                    rhs_scale=w_scales[r][:],
-                    start=(r == 0),
-                    stop=(r == ROUNDS - 1),
-                )
+                mx_pass(r, a)
 
         x_sb = const.tile([P, B_TILES, IN], BF16)
         nc.sync.dma_start(out=x_sb[:], in_=x.rearrange("(p a) k -> p a k", a=B_TILES))
@@ -258,10 +273,10 @@ def tile_networkprc_pa_k_kernel(tc, x, centres, sigmas, w1, b1, out):
 
         acc = [accps.tile([P, CENT], F32, name="acc%d" % a) for a in range(B_TILES)]
 
-        for i in range(ROUNDS + 5):
+        for i in range(ROUNDS):
             for stage, r, part in (
-                (mx_passes, i - 5, ()),
                 (products, i - 1, (3,)),
+                (mx_passes, i - 5, ()),
                 (products, i, (0,)),
                 (p_quantise, i - 3, ()),
                 (w_quantise, i - 2, ()),
@@ -289,6 +304,32 @@ def tile_networkprc_pa_k_kernel(tc, x, centres, sigmas, w1, b1, out):
                 ahead = r == 0 and part == (0,) and stage in (products, distances)
                 if 0 <= r < ROUNDS and not ahead:
                     stage(r, *part)
+
+        last = ROUNDS - 1
+        products(last, 3)
+        distances(last, 3)
+        mx_passes(last - 4)
+        exponentials(last, 0)
+        w_copy(last, 1)
+        for t in range(1, PACK):
+            exponentials(last, t)
+        p_quantise(last - 2)
+        w_quantise(last - 1)
+        mx_passes(last - 3)
+        regroup(last - 1)
+        w_quantise(last)
+        p_quantise(last - 1)
+        mx_passes(last - 2)
+        mx_passes(last - 1)
+        grp[last] = gpool.tile([P, B, PACK], BF16, name="grp_last", align_bytes=64)
+        p_codes[last] = pcodes.tile([P, B], U32, name="p_codes", tag="p_codes", align_bytes=64)
+        p_scales[last] = pcodes.tile([P, B], U8, name="p_scales", tag="p_scales", align_bytes=64)
+        for a in range(B_TILES + 1):
+            if a < B_TILES:
+                regroup_vector(last, a * P, (a + 1) * P)
+            if a > 0:
+                quantise_block(last, a - 1)
+                mx_pass(last, a - 1)
 
         res = const.tile([P, B_TILES, CENT], F32)
         for a in range(B_TILES):

@@ -24,9 +24,10 @@ C_TILES = CENT // P
 W_AHEAD = 6
 PAIRS = K_PASS // 2
 CEN_LOADS = 16
-NORMS_AHEAD = 24
+NORMS_AHEAD = 32
 VECTOR_ROUNDS = 2
-GPSIMD_COLS = 416
+FINISH_LAG = 3
+GPSIMD_COLS = 400
 
 FLOPS = 2 * B * HID * (IN + CENT)
 
@@ -42,11 +43,10 @@ def tile_networkprc_pa_k_kernel(tc, x, centres, sigmas, w1, b1, out):
         cpool = ctx.enter_context(tc.tile_pool(name="cpool", bufs=4))
         junk = ctx.enter_context(tc.tile_pool(name="junk", bufs=4))
         dpool = ctx.enter_context(tc.tile_pool(name="dpool", bufs=6))
-        phpool = ctx.enter_context(tc.tile_pool(name="phpool", bufs=3))
+        phpool = ctx.enter_context(tc.tile_pool(name="phpool", bufs=4))
         gpool = ctx.enter_context(tc.tile_pool(name="gpool", bufs=1))
         accps = ctx.enter_context(tc.psum_pool(name="accps", bufs=1))
-        spsum = ctx.enter_context(tc.psum_pool(name="spsum", bufs=2))
-        tpsum = ctx.enter_context(tc.psum_pool(name="tpsum", bufs=2))
+        psum = ctx.enter_context(tc.psum_pool(name="psum", bufs=4))
         ctx.enter_context(tc.manual_schedule())
 
         w1_v = w1.rearrange("(ct c) j -> c ct j", c=P)
@@ -86,7 +86,7 @@ def tile_networkprc_pa_k_kernel(tc, x, centres, sigmas, w1, b1, out):
         def w_transposes(r, h):
             if h == 0 and r + W_AHEAD < ROUNDS:
                 load_w(r + W_AHEAD)
-            wT_ps[r, h] = tpsum.tile([P, 2, 2 * P], F32, name="wT_ps", tag="t_ps")
+            wT_ps[r, h] = psum.tile([P, 2, 2 * P], F32, name="wT_ps", tag="work")
             for u in range(2):
                 for q in range(2):
                     words = w_sb[r][:, 2 * h + q, :].bitcast(F32)
@@ -112,7 +112,7 @@ def tile_networkprc_pa_k_kernel(tc, x, centres, sigmas, w1, b1, out):
             return cen_sb[:, r, t, :]
 
         def c_transposes(r):
-            cT_ps[r] = tpsum.tile([P, PACK, P], BF16, name="cT_ps", tag="t_ps")
+            cT_ps[r] = psum.tile([P, PACK, P], BF16, name="cT_ps", tag="work")
             for t in range(PACK):
                 nc.tensor.transpose(cT_ps[r][:, t, :], centre_tile(r, t), ident_bf[:])
 
@@ -133,7 +133,7 @@ def tile_networkprc_pa_k_kernel(tc, x, centres, sigmas, w1, b1, out):
                 c_norm(n)
 
         def products(r, t):
-            s_ps[r, t] = spsum.tile([P, B], F32, name="s_ps", tag="s_ps")
+            s_ps[r, t] = psum.tile([P, B], F32, name="s_ps", tag="work")
             nc.tensor.matmul(s_ps[r, t][:], lhsT=cT[r][:, t, :], rhs=xT2[:], start=True, stop=True)
 
         def distances(r, t):
@@ -147,11 +147,13 @@ def tile_networkprc_pa_k_kernel(tc, x, centres, sigmas, w1, b1, out):
                 op1=ALU.subtract,
             )
 
-        def exponentials(r, t):
-            if t == 0:
+        def exponentials(r, t, first=0, last=B):
+            if t == 0 and first == 0:
                 ph[r] = phpool.tile([P, PACK, B], BF16, name="ph", tag="ph")
             col = PACK * r + t
-            nc.scalar.activation(out=ph[r][:, t, :], in_=d2[r, t][:], func=ACT.Exp, scale=negs2[:, col : col + 1])
+            nc.scalar.activation(
+                out=ph[r][:, t, first:last], in_=d2[r, t][:, first:last], func=ACT.Exp, scale=negs2[:, col : col + 1]
+            )
 
         def regroup_vector(r, first, last):
             nc.vector.tensor_scalar(
@@ -228,7 +230,7 @@ def tile_networkprc_pa_k_kernel(tc, x, centres, sigmas, w1, b1, out):
 
         c2 = const.tile([P, ROUNDS * PACK], F32)
 
-        xT_ps = tpsum.tile([P, B_TILES, P], BF16, tag="t_ps")
+        xT_ps = psum.tile([P, B_TILES, P], BF16, tag="work")
         for a in range(B_TILES):
             nc.tensor.transpose(xT_ps[:, a, :], x_sb[:, a, :], ident_bf[:])
         xT2 = const.tile([P, B], BF16)
@@ -244,7 +246,7 @@ def tile_networkprc_pa_k_kernel(tc, x, centres, sigmas, w1, b1, out):
         for n in range(PACK):
             c_norm(n)
 
-        x2_ps = spsum.tile([P, B], F32, tag="s_ps")
+        x2_ps = psum.tile([P, B], F32, tag="work")
         for a in range(B_TILES):
             nc.tensor.transpose(x2_ps[:, a * P : (a + 1) * P], x2col[:, a : a + 1].to_broadcast([P, P]), ident_f32[:])
         x2 = const.tile([P, B], F32)
@@ -252,7 +254,7 @@ def tile_networkprc_pa_k_kernel(tc, x, centres, sigmas, w1, b1, out):
 
         products(0, 0)
 
-        sigT_ps = tpsum.tile([P, 2, P], F32, tag="t_ps")
+        sigT_ps = psum.tile([P, 2, P], F32, tag="work")
         for u in range(2):
             nc.tensor.transpose(sigT_ps[:, u, :], sig_nat[:].bitcast(F32)[:, u:PAIRS:2], ident_f32[:])
         distances(0, 0)
@@ -268,71 +270,61 @@ def tile_networkprc_pa_k_kernel(tc, x, centres, sigmas, w1, b1, out):
 
         for n in range(PACK, NORMS_AHEAD):
             c_norm(n)
-        c_transposes(1)
-        c_copy(1)
 
         acc = [accps.tile([P, CENT], F32, name="acc%d" % a) for a in range(B_TILES)]
 
-        for i in range(ROUNDS):
+        last = ROUNDS - 1
+        blocks = (exponentials, regroup, p_quantise, mx_passes)
+        for i in range(ROUNDS + 6):
             for stage, r, part in (
-                (products, i - 1, (3,)),
-                (mx_passes, i - 5, ()),
-                (products, i, (0,)),
-                (p_quantise, i - 3, ()),
-                (w_quantise, i - 2, ()),
-                (regroup, i - 2, ()),
-                (distances, i - 1, (3,)),
-                (distances, i, (0,)),
-                (exponentials, i - 1, (0,)),
-                (norms, i, (0,)),
-                (w_copy, i - 1, (1,)),
                 (w_transposes, i, (0,)),
-                (c_transposes, i + 2, ()),
+                (w_transposes, i, (1,)),
+                (c_transposes, i + 1, ()),
+                (exponentials, i - 1, (0,)),
+                (w_copy, i, (0,)),
+                (p_quantise, i - 3, ()),
+                (w_quantise, i - 1, ()),
+                (regroup, i - 2, ()),
+                (w_copy, i, (1,)),
+                (products, i, (0,)),
                 (products, i, (1,)),
                 (products, i, (2,)),
-                (c_copy, i + 2, ()),
+                (c_copy, i + 1, ()),
+                (exponentials, i - 1, (1,)),
+                (norms, i, (0,)),
+                (products, i, (3,)),
+                (exponentials, i - 1, (2,)),
+                (norms, i, (1,)),
+                (exponentials, i - 1, (3,)),
+                (norms, i, (2,)),
+                (mx_passes, i - 4, ()),
+                (distances, i, (0,)),
                 (distances, i, (1,)),
                 (distances, i, (2,)),
-                (exponentials, i - 1, (1,)),
-                (norms, i, (1,)),
-                (exponentials, i - 1, (2,)),
-                (w_copy, i, (0,)),
-                (w_transposes, i, (1,)),
-                (norms, i, (2,)),
-                (exponentials, i - 1, (3,)),
+                (distances, i, (3,)),
             ):
                 ahead = r == 0 and part == (0,) and stage in (products, distances)
-                if 0 <= r < ROUNDS and not ahead:
+                if 0 <= r < ROUNDS and not ahead and not (r == last and stage in blocks):
                     stage(r, *part)
 
-        last = ROUNDS - 1
-        products(last, 3)
-        distances(last, 3)
-        mx_passes(last - 4)
-        exponentials(last, 0)
-        w_copy(last, 1)
-        for t in range(1, PACK):
-            exponentials(last, t)
-        p_quantise(last - 2)
-        w_quantise(last - 1)
-        mx_passes(last - 3)
-        regroup(last - 1)
-        w_quantise(last)
-        p_quantise(last - 1)
-        mx_passes(last - 2)
-        mx_passes(last - 1)
-        grp[last] = gpool.tile([P, B, PACK], BF16, name="grp_last", align_bytes=64)
-        p_codes[last] = pcodes.tile([P, B], U32, name="p_codes", tag="p_codes", align_bytes=64)
-        p_scales[last] = pcodes.tile([P, B], U8, name="p_scales", tag="p_scales", align_bytes=64)
-        for a in range(B_TILES + 1):
-            if a < B_TILES:
-                regroup_vector(last, a * P, (a + 1) * P)
-            if a > 0:
-                quantise_block(last, a - 1)
-                mx_pass(last, a - 1)
-
         res = const.tile([P, B_TILES, CENT], F32)
-        for a in range(B_TILES):
+
+        def finish(a):
             nc.vector.tensor_tensor(out=res[:, a, :], in0=acc[a][:], in1=b1_bc[:], op=ALU.add)
             nc.scalar.activation(out=res[:, a, :], in_=res[:, a, :], func=ACT.Relu)
             nc.sync.dma_start(out=out_v[:, a, :], in_=res[:, a, :])
+
+        for a in range(B_TILES):
+            for t in range(PACK):
+                exponentials(last, t, a * P, (a + 1) * P)
+        grp[last] = gpool.tile([P, B, PACK], BF16, name="grp_last", align_bytes=64)
+        p_codes[last] = pcodes.tile([P, B], U32, name="p_codes", tag="p_codes", align_bytes=64)
+        p_scales[last] = pcodes.tile([P, B], U8, name="p_scales", tag="p_scales", align_bytes=64)
+        for a in range(B_TILES + FINISH_LAG):
+            if a < B_TILES:
+                regroup_vector(last, a * P, (a + 1) * P)
+            if 0 < a <= B_TILES:
+                quantise_block(last, a - 1)
+                mx_pass(last, a - 1)
+            if a >= FINISH_LAG:
+                finish(a - FINISH_LAG)

@@ -24,9 +24,11 @@ C_TILES = CENT // P
 W_AHEAD = 6
 PAIRS = K_PASS // 2
 CEN_LOADS = 16
-NORMS_AHEAD = 32
+NORMS_AHEAD = 20
 VECTOR_ROUNDS = 2
 FINISH_LAG = 3
+X2_TILE = 3
+X2_ROUNDS = range(1, ROUNDS - 1)
 GPSIMD_COLS = 400
 
 FLOPS = 2 * B * HID * (IN + CENT)
@@ -126,17 +128,46 @@ def tile_networkprc_pa_k_kernel(tc, x, centres, sigmas, w1, b1, out):
                 out=squares[:], in_=centre_tile(n // PACK, n % PACK), func=ACT.Square, accum_out=c2[:, n : n + 1]
             )
 
-        def norms(i, k):
+        def c_norm_v(n):
+            centre = centre_tile(n // PACK, n % PACK)
+            squares = junk.tile([P, IN], BF16, name="squares_v", tag="squares_v")
+            nc.vector.scalar_tensor_tensor(
+                out=squares[:], in0=centre, scalar=1.0, in1=centre, op0=ALU.mult, op1=ALU.mult, accum_out=c2[:, n : n + 1]
+            )
+
+        def step_norms(i):
             left = ROUNDS * PACK - NORMS_AHEAD
             first, last = (NORMS_AHEAD + left * j // (ROUNDS - 1) for j in (i, i + 1))
-            for n in range(first + k, min(last, ROUNDS * PACK), 3):
+            return range(first, min(last, ROUNDS * PACK))
+
+        def norms_v(i):
+            for n in step_norms(i)[0:1]:
+                c_norm_v(n)
+
+        def norms(i, k):
+            for n in step_norms(i)[1 + k :: 3]:
                 c_norm(n)
+
+        def by_tensor(r, t):
+            return t == X2_TILE and r in X2_ROUNDS
 
         def products(r, t):
             s_ps[r, t] = psum.tile([P, B], F32, name="s_ps", tag="work")
-            nc.tensor.matmul(s_ps[r, t][:], lhsT=cT[r][:, t, :], rhs=xT2[:], start=True, stop=True)
+            extra = by_tensor(r, t)
+            nc.tensor.matmul(s_ps[r, t][:], lhsT=cT[r][:, t, :], rhs=xT2[:], start=True, stop=not extra)
+            if extra:
+                nc.tensor.matmul(s_ps[r, t][:], lhsT=minus[:], rhs=x2rows[:], start=False, stop=True)
+
+        def biases(r):
+            col = PACK * r + X2_TILE
+            if by_tensor(r, X2_TILE):
+                nc.gpsimd.tensor_tensor(
+                    out=bias[:, r : r + 1], in0=negs2[:, col : col + 1], in1=c2[:, col : col + 1], op=ALU.mult
+                )
 
         def distances(r, t):
+            if by_tensor(r, t):
+                return
             d2[r, t] = dpool.tile([P, B], F32, name="d2", tag="d2")
             nc.vector.scalar_tensor_tensor(
                 out=d2[r, t][:],
@@ -148,12 +179,21 @@ def tile_networkprc_pa_k_kernel(tc, x, centres, sigmas, w1, b1, out):
             )
 
         def exponentials(r, t, first=0, last=B):
-            if t == 0 and first == 0:
+            if r not in ph:
                 ph[r] = phpool.tile([P, PACK, B], BF16, name="ph", tag="ph")
             col = PACK * r + t
-            nc.scalar.activation(
-                out=ph[r][:, t, first:last], in_=d2[r, t][:, first:last], func=ACT.Exp, scale=negs2[:, col : col + 1]
-            )
+            if by_tensor(r, t):
+                nc.scalar.activation(
+                    out=ph[r][:, t, first:last],
+                    in_=s_ps[r, t][:, first:last],
+                    func=ACT.Exp,
+                    scale=s2[:, col : col + 1],
+                    bias=bias[:, r : r + 1],
+                )
+            else:
+                nc.scalar.activation(
+                    out=ph[r][:, t, first:last], in_=d2[r, t][:, first:last], func=ACT.Exp, scale=negs2[:, col : col + 1]
+                )
 
         def regroup_vector(r, first, last):
             nc.vector.tensor_scalar(
@@ -212,10 +252,10 @@ def tile_networkprc_pa_k_kernel(tc, x, centres, sigmas, w1, b1, out):
 
         x_sb = const.tile([P, B_TILES, IN], BF16)
         nc.sync.dma_start(out=x_sb[:], in_=x.rearrange("(p a) k -> p a k", a=B_TILES))
-        cen_sb = const.tile([P, ROUNDS, PACK, IN], BF16)
-        load_centres(0)
         sig_nat = const.tile([P, K_PASS], BF16)
         nc.vector.memset(sig_nat[:], 0.0)
+        cen_sb = const.tile([P, ROUNDS, PACK, IN], BF16)
+        load_centres(0)
         nc.sync.dma_start(out=sig_nat[0:ROUNDS, :], in_=sigmas.rearrange("(r w) -> r w", w=K_PASS))
         load_centres(1)
         load_w(0)
@@ -252,24 +292,62 @@ def tile_networkprc_pa_k_kernel(tc, x, centres, sigmas, w1, b1, out):
         x2 = const.tile([P, B], F32)
         nc.vector.tensor_copy(out=x2[:], in_=x2_ps[:])
 
-        products(0, 0)
-
         sigT_ps = psum.tile([P, 2, P], F32, tag="work")
         for u in range(2):
             nc.tensor.transpose(sigT_ps[:, u, :], sig_nat[:].bitcast(F32)[:, u:PAIRS:2], ident_f32[:])
+
+        products(0, 0)
+        products(0, 1)
+        products(0, 2)
         distances(0, 0)
         sigT = const.tile([P, P], BF16)
         nc.vector.tensor_copy(
             out=sigT[:].bitcast(F32).rearrange("p (r u) -> p r u", u=2),
             in_=sigT_ps[:, :, 0:ROUNDS].rearrange("p u r -> p r u"),
         )
+        distances(0, 1)
         negs2 = const.tile([P, P], F32)
         nc.vector.scalar_tensor_tensor(
             out=negs2[:], in0=sigT[:], scalar=-1.0, in1=sigT[:], op0=ALU.mult, op1=ALU.mult
         )
-
+        products(0, 3)
         for n in range(PACK, NORMS_AHEAD):
             c_norm(n)
+        distances(0, 2)
+        exponentials(0, 0)
+        distances(0, 3)
+        exponentials(0, 1)
+        exponentials(0, 2)
+        exponentials(0, 3)
+
+        pieces = const.tile([P, B_TILES, P], BF16)
+        nc.gpsimd.memset(pieces[:], 0.0)
+        rest = x2col
+        for k in range(3):
+            piece = const.tile([P, B_TILES], BF16, name="piece%d" % k)
+            nc.gpsimd.tensor_copy(out=piece[:], in_=rest[:])
+            for a in range(B_TILES):
+                nc.gpsimd.tensor_copy(
+                    out=pieces[:, a, k * 32 : (k + 1) * 32], in_=piece[:, a : a + 1].to_broadcast([P, 32])
+                )
+            if k < 2:
+                left = const.tile([P, B_TILES], F32, name="left%d" % k)
+                nc.gpsimd.tensor_tensor(out=left[:], in0=rest[:], in1=piece[:], op=ALU.subtract)
+                rest = left
+        minus = const.tile([P, P], BF16)
+        nc.gpsimd.memset(minus[:], 0.0)
+        for k in range(3):
+            nc.gpsimd.memset(minus[k * 32 : k * 32 + 1, :], -1.0)
+        x2rows = const.tile([P, B], BF16)
+        bias = const.tile([P, ROUNDS], F32)
+        s2 = const.tile([P, P], F32)
+        nc.gpsimd.tensor_tensor(out=s2[:], in0=sigT[:], in1=sigT[:], op=ALU.mult)
+
+        def x2_rows(r):
+            rows_ps = psum.tile([P, B_TILES, P], BF16, name="rows_ps", tag="work")
+            for a in range(B_TILES):
+                nc.tensor.transpose(rows_ps[:, a, :], pieces[:, a, :], ident_bf[:])
+            nc.vector.tensor_copy(out=x2rows[:], in_=rows_ps[:].rearrange("p a i -> p (a i)"))
 
         acc = [accps.tile([P, CENT], F32, name="acc%d" % a) for a in range(B_TILES)]
 
@@ -277,33 +355,36 @@ def tile_networkprc_pa_k_kernel(tc, x, centres, sigmas, w1, b1, out):
         blocks = (exponentials, regroup, p_quantise, mx_passes)
         for i in range(ROUNDS + 6):
             for stage, r, part in (
-                (w_transposes, i, (0,)),
-                (w_transposes, i, (1,)),
-                (c_transposes, i + 1, ()),
+                (w_transposes, i - 1, (0,)),
+                (x2_rows, 0 if i == 0 else -1, ()),
                 (exponentials, i - 1, (0,)),
-                (w_copy, i, (0,)),
+                (norms_v, i, ()),
                 (p_quantise, i - 3, ()),
-                (w_quantise, i - 1, ()),
-                (regroup, i - 2, ()),
-                (w_copy, i, (1,)),
-                (products, i, (0,)),
-                (products, i, (1,)),
-                (products, i, (2,)),
-                (c_copy, i + 1, ()),
-                (exponentials, i - 1, (1,)),
-                (norms, i, (0,)),
-                (products, i, (3,)),
-                (exponentials, i - 1, (2,)),
-                (norms, i, (1,)),
-                (exponentials, i - 1, (3,)),
+                (biases, i, ()),
+                (w_transposes, i - 1, (1,)),
+                (w_copy, i - 1, (0,)),
+                (w_copy, i - 1, (1,)),
+                (w_quantise, i - 2, ()),
+                (c_transposes, i + 1, ()),
                 (norms, i, (2,)),
-                (mx_passes, i - 4, ()),
-                (distances, i, (0,)),
-                (distances, i, (1,)),
-                (distances, i, (2,)),
+                (products, i, (3,)),
+                (regroup, i - 2, ()),
+                (products, i, (0,)),
                 (distances, i, (3,)),
+                (c_copy, i + 1, ()),
+                (exponentials, i, (3,)),
+                (products, i, (1,)),
+                (distances, i, (0,)),
+                (norms, i, (0,)),
+                (exponentials, i - 1, (2,)),
+                (products, i, (2,)),
+                (mx_passes, i - 4, ()),
+                (norms, i, (1,)),
+                (distances, i, (1,)),
+                (exponentials, i - 1, (1,)),
+                (distances, i, (2,)),
             ):
-                ahead = r == 0 and part == (0,) and stage in (products, distances)
+                ahead = r == 0 and stage in (products, distances, exponentials)
                 if 0 <= r < ROUNDS and not ahead and not (r == last and stage in blocks):
                     stage(r, *part)
 

from contextlib import ExitStack

import concourse.mybir as mybir
from concourse.masks import make_identity

F32 = mybir.dt.float32
BF16 = mybir.dt.bfloat16
U32 = mybir.dt.uint32
U8 = mybir.dt.uint8
FP8X4 = mybir.dt.float8_e4m3fn_x4
ACT = mybir.ActivationFunctionType
ALU = mybir.AluOpType

P = 128
B = 512
IN = 128
HID = 16384
CENT = 512
PACK = 4
K_PASS = P * PACK
ROUNDS = HID // K_PASS
B_TILES = B // P
C_TILES = CENT // P
W_AHEAD = 6
PAIRS = K_PASS // 2
CEN_LOADS = 16
NORMS_AHEAD = 20
VECTOR_ROUNDS = 2
FINISH_LAG = 3
X2_TILE = 3
X2_ROUNDS = range(1, ROUNDS - 1)
GPSIMD_COLS = 400

FLOPS = 2 * B * HID * (IN + CENT)


def tile_networkprc_pa_k_kernel(tc, x, centres, sigmas, w1, b1, out):
    nc = tc.nc
    with ExitStack() as ctx:
        const = ctx.enter_context(tc.tile_pool(name="const", bufs=1))
        wload = ctx.enter_context(tc.tile_pool(name="wload", bufs=W_AHEAD + 1))
        wgroup = ctx.enter_context(tc.tile_pool(name="wgroup", bufs=3))
        wcodes = ctx.enter_context(tc.tile_pool(name="wcodes", bufs=6))
        pcodes = ctx.enter_context(tc.tile_pool(name="pcodes", bufs=3))
        cpool = ctx.enter_context(tc.tile_pool(name="cpool", bufs=4))
        junk = ctx.enter_context(tc.tile_pool(name="junk", bufs=4))
        dpool = ctx.enter_context(tc.tile_pool(name="dpool", bufs=6))
        phpool = ctx.enter_context(tc.tile_pool(name="phpool", bufs=4))
        gpool = ctx.enter_context(tc.tile_pool(name="gpool", bufs=1))
        accps = ctx.enter_context(tc.psum_pool(name="accps", bufs=1))
        psum = ctx.enter_context(tc.psum_pool(name="psum", bufs=4))
        ctx.enter_context(tc.manual_schedule())

        w1_v = w1.rearrange("(ct c) j -> c ct j", c=P)
        cen_v = centres.rearrange("(r p t) k -> p r t k", p=P, t=PACK)
        out_v = out.rearrange("(p a) c -> p a c", a=B_TILES)

        w_sb = {}
        wT_ps = {}
        wgrp = {}
        w_codes = {}
        w_scales = {}
        cT_ps = {}
        cT = {}
        s_ps = {}
        d2 = {}
        ph = {}
        grp = {}
        p_codes = {}
        p_scales = {}

        ident_bf = const.tile([P, P], BF16)
        make_identity(nc, ident_bf[:])
        ident_f32 = const.tile([P, P], F32)
        make_identity(nc, ident_f32[:])

        def load_w(r):
            w_sb[r] = wload.tile([P, C_TILES, K_PASS], BF16, name="w_sb", tag="w_sb")
            nc.sync.dma_start(out=w_sb[r][:], in_=w1_v[:, :, r * K_PASS : (r + 1) * K_PASS])

        def load_centres(n):
            step = ROUNDS // CEN_LOADS
            nc.sync.dma_start(
                out=cen_sb[:, n * step : (n + 1) * step, :, :],
                in_=cen_v[:, n * step : (n + 1) * step, :, :],
            )

        def w_transposes(r, h):
            if h == 0 and r + W_AHEAD < ROUNDS:
                load_w(r + W_AHEAD)
            wT_ps[r, h] = psum.tile([P, 2, 2 * P], F32, name="wT_ps", tag="work")
            for u in range(2):
                for q in range(2):
                    words = w_sb[r][:, 2 * h + q, :].bitcast(F32)
                    nc.tensor.transpose(
                        wT_ps[r, h][:, u, q * P : (q + 1) * P], words[:, u:PAIRS:2], ident_f32[:]
                    )

        def w_copy(r, h):
            if h == 0:
                wgrp[r] = wgroup.tile([P, CENT * PACK], BF16, name="wgrp", tag="wgrp", align_bytes=64)
            words = wgrp[r][:].bitcast(F32).rearrange("p (c u) -> p c u", u=2)
            nc.scalar.copy(
                out=words[:, h * 2 * P : (h + 1) * 2 * P, :],
                in_=wT_ps[r, h][:].rearrange("p u c -> p c u"),
            )

        def w_quantise(r):
            w_codes[r] = wcodes.tile([P, CENT], U32, name="w_codes", tag="w_codes", align_bytes=64)
            w_scales[r] = wcodes.tile([P, CENT], U8, name="w_scales", tag="w_scales", align_bytes=64)
            nc.vector.quantize_mx(out=w_codes[r][:].bitcast(FP8X4), scales=w_scales[r][:], in_=wgrp[r][:])

        def centre_tile(r, t):
            return cen_sb[:, r, t, :]

        def c_transposes(r):
            cT_ps[r] = psum.tile([P, PACK, P], BF16, name="cT_ps", tag="work")
            for t in range(PACK):
                nc.tensor.transpose(cT_ps[r][:, t, :], centre_tile(r, t), ident_bf[:])

        def c_copy(r):
            cT[r] = cpool.tile([P, PACK, P], BF16, name="cT", tag="cT")
            nc.vector.tensor_copy(out=cT[r][:], in_=cT_ps[r][:])

        def c_norm(n):
            squares = junk.tile([P, IN], BF16, name="squares", tag="squares")
            nc.scalar.activation(
                out=squares[:], in_=centre_tile(n // PACK, n % PACK), func=ACT.Square, accum_out=c2[:, n : n + 1]
            )

        def c_norm_v(n):
            centre = centre_tile(n // PACK, n % PACK)
            squares = junk.tile([P, IN], BF16, name="squares_v", tag="squares_v")
            nc.vector.scalar_tensor_tensor(
                out=squares[:], in0=centre, scalar=1.0, in1=centre, op0=ALU.mult, op1=ALU.mult, accum_out=c2[:, n : n + 1]
            )

        def step_norms(i):
            left = ROUNDS * PACK - NORMS_AHEAD
            first, last = (NORMS_AHEAD + left * j // (ROUNDS - 1) for j in (i, i + 1))
            return range(first, min(last, ROUNDS * PACK))

        def norms_v(i):
            for n in step_norms(i)[0:1]:
                c_norm_v(n)

        def norms(i, k):
            for n in step_norms(i)[1 + k :: 3]:
                c_norm(n)

        def by_tensor(r, t):
            return t == X2_TILE and r in X2_ROUNDS

        def products(r, t):
            s_ps[r, t] = psum.tile([P, B], F32, name="s_ps", tag="work")
            extra = by_tensor(r, t)
            nc.tensor.matmul(s_ps[r, t][:], lhsT=cT[r][:, t, :], rhs=xT2[:], start=True, stop=not extra)
            if extra:
                nc.tensor.matmul(s_ps[r, t][:], lhsT=minus[:], rhs=x2rows[:], start=False, stop=True)

        def biases(r):
            col = PACK * r + X2_TILE
            if by_tensor(r, X2_TILE):
                nc.gpsimd.tensor_tensor(
                    out=bias[:, r : r + 1], in0=negs2[:, col : col + 1], in1=c2[:, col : col + 1], op=ALU.mult
                )

        def distances(r, t):
            if by_tensor(r, t):
                return
            d2[r, t] = dpool.tile([P, B], F32, name="d2", tag="d2")
            nc.vector.scalar_tensor_tensor(
                out=d2[r, t][:],
                in0=x2[:],
                scalar=c2[:, PACK * r + t : PACK * r + t + 1],
                in1=s_ps[r, t][:],
                op0=ALU.add,
                op1=ALU.subtract,
            )

        def exponentials(r, t, first=0, last=B):
            if r not in ph:
                ph[r] = phpool.tile([P, PACK, B], BF16, name="ph", tag="ph")
            col = PACK * r + t
            if by_tensor(r, t):
                nc.scalar.activation(
                    out=ph[r][:, t, first:last],
                    in_=s_ps[r, t][:, first:last],
                    func=ACT.Exp,
                    scale=s2[:, col : col + 1],
                    bias=bias[:, r : r + 1],
                )
            else:
                nc.scalar.activation(
                    out=ph[r][:, t, first:last], in_=d2[r, t][:, first:last], func=ACT.Exp, scale=negs2[:, col : col + 1]
                )

        def regroup_vector(r, first, last):
            nc.vector.tensor_scalar(
                out=grp[r][:, first:last, :].rearrange("p (c i) t -> p c t i", i=4),
                in0=ph[r][:, :, first:last].rearrange("p t (c i) -> p c t i", i=4),
                scalar1=1.0,
                scalar2=None,
                op0=ALU.min,
            )

        def regroup(r):
            cut = GPSIMD_COLS if r < ROUNDS - VECTOR_ROUNDS else 0
            grp[r] = gpool.tile([P, B, PACK], BF16, name="grp", tag="grp", align_bytes=64)
            regroup_vector(r, cut, B)
            if cut == 0:
                return
            nc.gpsimd.tensor_scalar(
                out=grp[r][:, 0:cut, :],
                in0=ph[r][:, :, 0:cut].rearrange("p t n -> p n t"),
                scalar1=1.0,
                scalar2=0.0,
                op0=ALU.min,
                op1=ALU.max,
            )

        def p_quantise(r):
            p_codes[r] = pcodes.tile([P, B], U32, name="p_codes", tag="p_codes", align_bytes=64)
            p_scales[r] = pcodes.tile([P, B], U8, name="p_scales", tag="p_scales", align_bytes=64)
            nc.vector.quantize_mx(
                out=p_codes[r][:].bitcast(FP8X4), scales=p_scales[r][:], in_=grp[r][:].rearrange("p n t -> p (n t)")
            )

        def quantise_block(r, a):
            cols = slice(a * P, (a + 1) * P)
            nc.vector.quantize_mx(
                out=p_codes[r][:, cols].bitcast(FP8X4),
                scales=p_scales[r][:, cols],
                in_=grp[r][:, cols, :].rearrange("p n t -> p (n t)"),
            )

        def mx_pass(r, a):
            cols = slice(a * P, (a + 1) * P)
            nc.tensor.matmul_mx(
                out=acc[a][:],
                lhsT=p_codes[r][:, cols].bitcast(FP8X4),
                lhsT_scale=p_scales[r][:, cols],
                rhs=w_codes[r][:].bitcast(FP8X4),
                rhs_scale=w_scales[r][:],
                start=(r == 0),
                stop=(r == ROUNDS - 1),
            )

        def mx_passes(r):
            for a in range(B_TILES):
                mx_pass(r, a)

        x_sb = const.tile([P, B_TILES, IN], BF16)
        nc.sync.dma_start(out=x_sb[:], in_=x.rearrange("(p a) k -> p a k", a=B_TILES))
        sig_nat = const.tile([P, K_PASS], BF16)
        nc.vector.memset(sig_nat[:], 0.0)
        cen_sb = const.tile([P, ROUNDS, PACK, IN], BF16)
        load_centres(0)
        nc.sync.dma_start(out=sig_nat[0:ROUNDS, :], in_=sigmas.rearrange("(r w) -> r w", w=K_PASS))
        load_centres(1)
        load_w(0)
        load_centres(2)
        for n in range(1, W_AHEAD):
            load_centres(n + 2)
            load_w(n)
        for n in range(W_AHEAD + 2, CEN_LOADS):
            load_centres(n)
        b1_bc = const.tile([P, CENT], BF16)
        nc.sync.dma_start(out=b1_bc[:], in_=b1.partition_broadcast(P))

        c2 = const.tile([P, ROUNDS * PACK], F32)

        xT_ps = psum.tile([P, B_TILES, P], BF16, tag="work")
        for a in range(B_TILES):
            nc.tensor.transpose(xT_ps[:, a, :], x_sb[:, a, :], ident_bf[:])
        xT2 = const.tile([P, B], BF16)
        nc.vector.tensor_scalar(
            out=xT2[:], in0=xT_ps[:].rearrange("p a i -> p (a i)"), scalar1=2.0, scalar2=None, op0=ALU.mult
        )
        x2col = const.tile([P, B_TILES], F32)
        for a in range(B_TILES):
            squares = junk.tile([P, IN], BF16, name="squares", tag="squares")
            nc.scalar.activation(out=squares[:], in_=x_sb[:, a, :], func=ACT.Square, accum_out=x2col[:, a : a + 1])
        c_transposes(0)
        c_copy(0)
        for n in range(PACK):
            c_norm(n)

        x2_ps = psum.tile([P, B], F32, tag="work")
        for a in range(B_TILES):
            nc.tensor.transpose(x2_ps[:, a * P : (a + 1) * P], x2col[:, a : a + 1].to_broadcast([P, P]), ident_f32[:])
        x2 = const.tile([P, B], F32)
        nc.vector.tensor_copy(out=x2[:], in_=x2_ps[:])

        sigT_ps = psum.tile([P, 2, P], F32, tag="work")
        for u in range(2):
            nc.tensor.transpose(sigT_ps[:, u, :], sig_nat[:].bitcast(F32)[:, u:PAIRS:2], ident_f32[:])

        products(0, 0)
        products(0, 1)
        products(0, 2)
        distances(0, 0)
        sigT = const.tile([P, P], BF16)
        nc.vector.tensor_copy(
            out=sigT[:].bitcast(F32).rearrange("p (r u) -> p r u", u=2),
            in_=sigT_ps[:, :, 0:ROUNDS].rearrange("p u r -> p r u"),
        )
        distances(0, 1)
        negs2 = const.tile([P, P], F32)
        nc.vector.scalar_tensor_tensor(
            out=negs2[:], in0=sigT[:], scalar=-1.0, in1=sigT[:], op0=ALU.mult, op1=ALU.mult
        )
        products(0, 3)
        for n in range(PACK, NORMS_AHEAD):
            c_norm(n)
        distances(0, 2)
        exponentials(0, 0)
        distances(0, 3)
        exponentials(0, 1)
        exponentials(0, 2)
        exponentials(0, 3)

        pieces = const.tile([P, B_TILES, P], BF16)
        nc.gpsimd.memset(pieces[:], 0.0)
        rest = x2col
        for k in range(3):
            piece = const.tile([P, B_TILES], BF16, name="piece%d" % k)
            nc.gpsimd.tensor_copy(out=piece[:], in_=rest[:])
            for a in range(B_TILES):
                nc.gpsimd.tensor_copy(
                    out=pieces[:, a, k * 32 : (k + 1) * 32], in_=piece[:, a : a + 1].to_broadcast([P, 32])
                )
            if k < 2:
                left = const.tile([P, B_TILES], F32, name="left%d" % k)
                nc.gpsimd.tensor_tensor(out=left[:], in0=rest[:], in1=piece[:], op=ALU.subtract)
                rest = left
        minus = const.tile([P, P], BF16)
        nc.gpsimd.memset(minus[:], 0.0)
        for k in range(3):
            nc.gpsimd.memset(minus[k * 32 : k * 32 + 1, :], -1.0)
        x2rows = const.tile([P, B], BF16)
        bias = const.tile([P, ROUNDS], F32)
        s2 = const.tile([P, P], F32)
        nc.gpsimd.tensor_tensor(out=s2[:], in0=sigT[:], in1=sigT[:], op=ALU.mult)

        def x2_rows(r):
            rows_ps = psum.tile([P, B_TILES, P], BF16, name="rows_ps", tag="work")
            for a in range(B_TILES):
                nc.tensor.transpose(rows_ps[:, a, :], pieces[:, a, :], ident_bf[:])
            nc.vector.tensor_copy(out=x2rows[:], in_=rows_ps[:].rearrange("p a i -> p (a i)"))

        acc = [accps.tile([P, CENT], F32, name="acc%d" % a) for a in range(B_TILES)]

        last = ROUNDS - 1
        blocks = (exponentials, regroup, p_quantise, mx_passes)
        for i in range(ROUNDS + 6):
            for stage, r, part in (
                (w_transposes, i - 1, (0,)),
                (x2_rows, 0 if i == 0 else -1, ()),
                (exponentials, i - 1, (0,)),
                (norms_v, i, ()),
                (p_quantise, i - 3, ()),
                (biases, i, ()),
                (w_transposes, i - 1, (1,)),
                (w_copy, i - 1, (0,)),
                (w_copy, i - 1, (1,)),
                (w_quantise, i - 2, ()),
                (c_transposes, i + 1, ()),
                (norms, i, (2,)),
                (products, i, (3,)),
                (regroup, i - 2, ()),
                (products, i, (0,)),
                (distances, i, (3,)),
                (c_copy, i + 1, ()),
                (exponentials, i, (3,)),
                (products, i, (1,)),
                (distances, i, (0,)),
                (norms, i, (0,)),
                (exponentials, i - 1, (2,)),
                (products, i, (2,)),
                (mx_passes, i - 4, ()),
                (norms, i, (1,)),
                (distances, i, (1,)),
                (exponentials, i - 1, (1,)),
                (distances, i, (2,)),
            ):
                ahead = r == 0 and stage in (products, distances, exponentials)
                if 0 <= r < ROUNDS and not ahead and not (r == last and stage in blocks):
                    stage(r, *part)

        res = const.tile([P, B_TILES, CENT], F32)

        def finish(a):
            nc.vector.tensor_tensor(out=res[:, a, :], in0=acc[a][:], in1=b1_bc[:], op=ALU.add)
            nc.scalar.activation(out=res[:, a, :], in_=res[:, a, :], func=ACT.Relu)
            nc.sync.dma_start(out=out_v[:, a, :], in_=res[:, a, :])

        for a in range(B_TILES):
            for t in range(PACK):
                exponentials(last, t, a * P, (a + 1) * P)
        grp[last] = gpool.tile([P, B, PACK], BF16, name="grp_last", align_bytes=64)
        p_codes[last] = pcodes.tile([P, B], U32, name="p_codes", tag="p_codes", align_bytes=64)
        p_scales[last] = pcodes.tile([P, B], U8, name="p_scales", tag="p_scales", align_bytes=64)
        for a in range(B_TILES + FINISH_LAG):
            if a < B_TILES:
                regroup_vector(last, a * P, (a + 1) * P)
            if 0 < a <= B_TILES:
                quantise_block(last, a - 1)
                mx_pass(last, a - 1)
            if a >= FINISH_LAG:
                finish(a - FINISH_LAG)
